import numpy as np
import ml_dtypes

BF16 = ml_dtypes.bfloat16


def bf(x):
    return np.asarray(x, np.float32).astype(BF16)


def f32(x):
    return np.asarray(x, np.float32)


def f64(x):
    return np.asarray(x).astype(np.float64)


def striped(idx):
    return np.tile(idx.reshape(-1, 16).T, (8, 1))


C, S, N = 128, 1024, 256
EPS = 1e-5
NEG_SLOPE = 0.01


def setup_inputs():
    return {
        "base": f32(np.random.standard_normal((C, S))),
        "x_self": f32(np.random.standard_normal((C, N))),
        "x_cycle": f32(np.random.standard_normal((C, N))),
        "x_pair": f32(np.random.standard_normal((C, N))),
        "x_hub": f32(np.random.standard_normal((C, N))),
        "w": bf(np.random.standard_normal((C, C)) / np.sqrt(C)),
        "ln_scale": f32(1.0 + 0.1 * np.random.standard_normal((C, 1))),
        "ln_shift": f32(0.1 * np.random.standard_normal((C, 1))),
        "offs": striped(np.random.permutation(S)[:N]),
    }


def reference(base, x_self, x_cycle, x_pair, x_hub, w, ln_scale, ln_shift, offs):
    idx = offs[:16].T.reshape(-1)
    agg = f64(x_self) + f64(x_cycle) + f64(x_pair) + f64(x_hub)
    h = f64(w).T @ agg
    mean = h.mean(axis=0, keepdims=True)
    var = np.square(h - mean).mean(axis=0, keepdims=True)
    v = (h - mean) / np.sqrt(var + EPS) * f64(ln_scale) + f64(ln_shift)
    slope = np.where(v >= 0.0, 1.0, NEG_SLOPE)
    out = f64(base).copy()
    out[:, idx] = v * slope
    return out

@@ -1,0 +1,94 @@
+import concourse.mybir as mybir
+from concourse.masks import make_identity
+
+F32 = mybir.dt.float32
+BF16 = mybir.dt.bfloat16
+U16 = mybir.dt.uint16
+ALU = mybir.AluOpType
+ACT = mybir.ActivationFunctionType
+
+C = 128
+S = 1024
+N = 256
+BLOCK = 128
+NBLOCKS = N // BLOCK
+EPS = 1e-5
+NEG_SLOPE = 0.01
+
+FLOPS = 2 * C * C * N
+
+
+def tile_modularfieldvortexlayer_kernel(
+    tc, base, x_self, x_cycle, x_pair, x_hub, w, ln_scale, ln_shift, offs, out
+):
+    nc = tc.nc
+    with (
+        tc.tile_pool(name="held", bufs=1) as held,
+        tc.psum_pool(name="psum", bufs=1) as psum,
+    ):
+        xs = held.tile([C, N], F32, name="xs")
+        xc = held.tile([C, N], F32, name="xc")
+        xp = held.tile([C, N], F32, name="xp")
+        xh = held.tile([C, N], F32, name="xh")
+        nc.sync.dma_start(xs[:], x_self)
+        nc.scalar.dma_start(xc[:], x_cycle)
+        nc.sync.dma_start(xp[:], x_pair)
+        nc.scalar.dma_start(xh[:], x_hub)
+
+        weights = held.tile([C, C], BF16, name="weights")
+        nc.scalar.dma_start(weights[:], w)
+        offsets = held.tile([C, N // 16], U16, name="offsets")
+        nc.sync.dma_start(offsets[:], offs)
+        window = held.tile([C, S], F32, name="window")
+        nc.sync.dma_start(window[:], base)
+        scale = held.tile([C, 1], F32, name="scale")
+        nc.gpsimd.dma_start(scale[:], ln_scale)
+        shift = held.tile([C, 1], F32, name="shift")
+        nc.gpsimd.dma_start(shift[:], ln_shift)
+
+        identity = held.tile([BLOCK, BLOCK], F32, name="identity")
+        make_identity(nc, identity[:])
+        eps = held.tile([BLOCK, 1], F32, name="eps")
+        nc.vector.memset(eps[:], EPS)
+        table_warmer = held.tile([BLOCK, 1], F32, name="table_warmer")
+        nc.scalar.activation(table_warmer[:], eps[:], ACT.Sqrt)
+
+        sum2 = held.tile([C, N], F32, name="sum2")
+        nc.vector.tensor_tensor(sum2[:], xs[:], xc[:], ALU.add)
+        sum3 = held.tile([C, N], F32, name="sum3")
+        nc.vector.tensor_tensor(sum3[:], sum2[:], xp[:], ALU.add)
+        agg = held.tile([C, N], BF16, name="agg")
+        nc.vector.tensor_tensor(agg[:], sum3[:], xh[:], ALU.add)
+
+        h_t = [psum.tile([BLOCK, C], F32, name=f"h_t{b}") for b in range(NBLOCKS)]
+        for b in range(NBLOCKS):
+            nc.tensor.matmul(
+                h_t[b][:], agg[:, b * BLOCK : (b + 1) * BLOCK], weights[:], start=True, stop=True
+            )
+
+        stats = held.tile([BLOCK, NBLOCKS, 6], F32, name="stats")
+        mean_var = held.tile([BLOCK, NBLOCKS, 2], F32, name="mean_var")
+        for b in range(NBLOCKS):
+            nc.vector.bn_stats(stats[:, b, :], h_t[b][:])
+        for b in range(NBLOCKS):
+            nc.vector.bn_aggr(mean_var[:, b, :], stats[:, b, :])
+        std = held.tile([BLOCK, NBLOCKS, 1], F32, name="std")
+        nc.scalar.activation(std[:], mean_var[:, :, 1:2], ACT.Sqrt, bias=eps[:])
+        rstd = held.tile([BLOCK, NBLOCKS, 1], F32, name="rstd")
+        nc.vector.reciprocal(rstd[:], std[:])
+
+        normed = psum.tile([C, N], F32, name="normed")
+        for b in range(NBLOCKS):
+            normed_t = held.tile([BLOCK, C], F32, name=f"normed_t{b}")
+            nc.vector.tensor_scalar(
+                normed_t[:], h_t[b][:], mean_var[:, b, 0:1], rstd[:, b, :], ALU.subtract, ALU.mult
+            )
+            nc.tensor.transpose(normed[:, b * BLOCK : (b + 1) * BLOCK], normed_t[:], identity[:])
+
+        v = held.tile([C, N], F32, name="v")
+        nc.vector.tensor_scalar(v[:], normed[:], scale[:], shift[:], ALU.mult, ALU.add)
+        slope = held.tile([C, N], F32, name="slope")
+        nc.vector.tensor_scalar(slope[:], v[:], 0.0, NEG_SLOPE, ALU.is_ge, ALU.max)
+        nc.vector.tensor_tensor(window[:].indirect(offsets[:]), v[:], slope[:], ALU.mult)
+
+        nc.sync.dma_start(out, window[:])

@@ -39,56 +39,66 @@ def tile_modularfieldvortexlayer_kernel(
         nc.scalar.dma_start(weights[:], w)
         offsets = held.tile([C, N // 16], U16, name="offsets")
         nc.sync.dma_start(offsets[:], offs)
+        scale_rows = held.tile([BLOCK, C], F32, name="scale_rows")
+        nc.scalar.dma_start(scale_rows[:], ln_scale.rearrange("m one -> (m one)").partition_broadcast(BLOCK))
+        shift = held.tile([C, 1], F32, name="shift")
+        nc.scalar.dma_start(shift[:], ln_shift)
         window = held.tile([C, S], F32, name="window")
         nc.sync.dma_start(window[:], base)
-        scale = held.tile([C, 1], F32, name="scale")
-        nc.gpsimd.dma_start(scale[:], ln_scale)
-        shift = held.tile([C, 1], F32, name="shift")
-        nc.gpsimd.dma_start(shift[:], ln_shift)
 
         identity = held.tile([BLOCK, BLOCK], F32, name="identity")
         make_identity(nc, identity[:])
+        neg_shift = held.tile([C, 1], F32, name="neg_shift")
+        nc.gpsimd.tensor_scalar(neg_shift[:], shift[:], -1.0, None, ALU.mult)
         eps = held.tile([BLOCK, 1], F32, name="eps")
         nc.vector.memset(eps[:], EPS)
         table_warmer = held.tile([BLOCK, 1], F32, name="table_warmer")
-        nc.scalar.activation(table_warmer[:], eps[:], ACT.Sqrt)
+        nc.scalar.activation(table_warmer[:], eps[:], ACT.Abs_reciprocal_sqrt)
 
         sum2 = held.tile([C, N], F32, name="sum2")
         nc.vector.tensor_tensor(sum2[:], xs[:], xc[:], ALU.add)
         sum3 = held.tile([C, N], F32, name="sum3")
         nc.vector.tensor_tensor(sum3[:], sum2[:], xp[:], ALU.add)
-        agg = held.tile([C, N], BF16, name="agg")
-        nc.vector.tensor_tensor(agg[:], sum3[:], xh[:], ALU.add)
 
-        h_t = [psum.tile([BLOCK, C], F32, name=f"h_t{b}") for b in range(NBLOCKS)]
+        h_t = []
         for b in range(NBLOCKS):
-            nc.tensor.matmul(
-                h_t[b][:], agg[:, b * BLOCK : (b + 1) * BLOCK], weights[:], start=True, stop=True
+            cols = slice(b * BLOCK, (b + 1) * BLOCK)
+            agg = held.tile([C, BLOCK], BF16, name=f"agg{b}")
+            nc.vector.tensor_tensor(agg[:], sum3[:, cols], xh[:, cols], ALU.add)
+            h_t.append(psum.tile([BLOCK, C], F32, name=f"h_t{b}"))
+            nc.tensor.matmul(h_t[b][:], agg[:], weights[:], start=True, stop=True)
+
+        mean_var = []
+        rstd = []
+        for b in range(NBLOCKS):
+            stats = held.tile([BLOCK, 6], F32, name=f"stats{b}")
+            nc.vector.bn_stats(stats[:], h_t[b][:])
+            mean_var.append(held.tile([BLOCK, 2], F32, name=f"mean_var{b}"))
+            nc.vector.bn_aggr(mean_var[b][:], stats[:])
+            rstd.append(held.tile([BLOCK, 1], F32, name=f"rstd{b}"))
+            nc.scalar.activation(rstd[b][:], mean_var[b][:, 1:2], ACT.Abs_reciprocal_sqrt, bias=eps[:])
+
+        centred_t = []
+        for b in range(NBLOCKS):
+            centred_t.append(held.tile([BLOCK, C], F32, name=f"centred_t{b}"))
+            nc.vector.scalar_tensor_tensor(
+                centred_t[b][:], h_t[b][:], mean_var[b][:, 0:1], scale_rows[:], ALU.subtract, ALU.mult
             )
 
-        stats = held.tile([BLOCK, NBLOCKS, 6], F32, name="stats")
-        mean_var = held.tile([BLOCK, NBLOCKS, 2], F32, name="mean_var")
+        u = []
         for b in range(NBLOCKS):
-            nc.vector.bn_stats(stats[:, b, :], h_t[b][:])
-        for b in range(NBLOCKS):
-            nc.vector.bn_aggr(mean_var[:, b, :], stats[:, b, :])
-        std = held.tile([BLOCK, NBLOCKS, 1], F32, name="std")
-        nc.scalar.activation(std[:], mean_var[:, :, 1:2], ACT.Sqrt, bias=eps[:])
-        rstd = held.tile([BLOCK, NBLOCKS, 1], F32, name="rstd")
-        nc.vector.reciprocal(rstd[:], std[:])
-
-        normed = psum.tile([C, N], F32, name="normed")
-        for b in range(NBLOCKS):
-            normed_t = held.tile([BLOCK, C], F32, name=f"normed_t{b}")
-            nc.vector.tensor_scalar(
-                normed_t[:], h_t[b][:], mean_var[:, b, 0:1], rstd[:, b, :], ALU.subtract, ALU.mult
-            )
-            nc.tensor.transpose(normed[:, b * BLOCK : (b + 1) * BLOCK], normed_t[:], identity[:])
+            u_t = held.tile([BLOCK, C], F32, name=f"u_t{b}")
+            nc.vector.tensor_scalar(u_t[:], centred_t[b][:], rstd[b][:], None, ALU.mult)
+            u.append(psum.tile([C, BLOCK], F32, name=f"u{b}"))
+            nc.tensor.transpose(u[b][:], u_t[:], identity[:])
 
         v = held.tile([C, N], F32, name="v")
-        nc.vector.tensor_scalar(v[:], normed[:], scale[:], shift[:], ALU.mult, ALU.add)
         slope = held.tile([C, N], F32, name="slope")
-        nc.vector.tensor_scalar(slope[:], v[:], 0.0, NEG_SLOPE, ALU.is_ge, ALU.max)
+        for b in range(NBLOCKS):
+            cols = slice(b * BLOCK, (b + 1) * BLOCK)
+            nc.vector.tensor_scalar(v[:, cols], u[b][:], shift[:], None, ALU.add)
+            nc.vector.tensor_scalar(slope[:, cols], u[b][:], neg_shift[:], NEG_SLOPE, ALU.is_ge, ALU.max)
+
         nc.vector.tensor_tensor(window[:].indirect(offsets[:]), v[:], slope[:], ALU.mult)
 
         nc.sync.dma_start(out, window[:])

@@ -34,26 +34,26 @@ def tile_modularfieldvortexlayer_kernel(
         nc.scalar.dma_start(xc[:], x_cycle)
         nc.sync.dma_start(xp[:], x_pair)
         nc.scalar.dma_start(xh[:], x_hub)
-
         weights = held.tile([C, C], BF16, name="weights")
-        nc.scalar.dma_start(weights[:], w)
+        nc.sync.dma_start(weights[:], w)
+        scale_rows = held.tile([BLOCK, C], F32, name="scale_rows")
+        nc.sync.dma_start(scale_rows[:], ln_scale.rearrange("m one -> (m one)").partition_broadcast(BLOCK))
+        shift = held.tile([C, 1], F32, name="shift")
+        nc.sync.dma_start(shift[:], ln_shift)
         offsets = held.tile([C, N // 16], U16, name="offsets")
         nc.sync.dma_start(offsets[:], offs)
-        scale_rows = held.tile([BLOCK, C], F32, name="scale_rows")
-        nc.scalar.dma_start(scale_rows[:], ln_scale.rearrange("m one -> (m one)").partition_broadcast(BLOCK))
-        shift = held.tile([C, 1], F32, name="shift")
-        nc.scalar.dma_start(shift[:], ln_shift)
         window = held.tile([C, S], F32, name="window")
         nc.sync.dma_start(window[:], base)
+
+        eps = held.tile([BLOCK, 1], F32, name="eps")
+        nc.vector.memset(eps[:], EPS)
+        table_warmer = held.tile([BLOCK, 1], F32, name="table_warmer")
+        nc.scalar.activation(table_warmer[:], eps[:], ACT.Abs_reciprocal_sqrt)
 
         identity = held.tile([BLOCK, BLOCK], F32, name="identity")
         make_identity(nc, identity[:])
         neg_shift = held.tile([C, 1], F32, name="neg_shift")
         nc.gpsimd.tensor_scalar(neg_shift[:], shift[:], -1.0, None, ALU.mult)
-        eps = held.tile([BLOCK, 1], F32, name="eps")
-        nc.vector.memset(eps[:], EPS)
-        table_warmer = held.tile([BLOCK, 1], F32, name="table_warmer")
-        nc.scalar.activation(table_warmer[:], eps[:], ACT.Abs_reciprocal_sqrt)
 
         sum2 = held.tile([C, N], F32, name="sum2")
         nc.vector.tensor_tensor(sum2[:], xs[:], xc[:], ALU.add)

@@ -36,69 +36,58 @@ def tile_modularfieldvortexlayer_kernel(
         nc.scalar.dma_start(xh[:], x_hub)
         weights = held.tile([C, C], BF16, name="weights")
         nc.sync.dma_start(weights[:], w)
-        scale_rows = held.tile([BLOCK, C], F32, name="scale_rows")
-        nc.sync.dma_start(scale_rows[:], ln_scale.rearrange("m one -> (m one)").partition_broadcast(BLOCK))
-        shift = held.tile([C, 1], F32, name="shift")
-        nc.sync.dma_start(shift[:], ln_shift)
         offsets = held.tile([C, N // 16], U16, name="offsets")
         nc.sync.dma_start(offsets[:], offs)
-        window = held.tile([C, S], F32, name="window")
-        nc.sync.dma_start(window[:], base)
+        scale = held.tile([C, 1], F32, name="scale")
+        nc.gpsimd.dma_start(scale[:], ln_scale)
+        shift = held.tile([C, 1], F32, name="shift")
+        nc.gpsimd.dma_start(shift[:], ln_shift)
 
         eps = held.tile([BLOCK, 1], F32, name="eps")
         nc.vector.memset(eps[:], EPS)
         table_warmer = held.tile([BLOCK, 1], F32, name="table_warmer")
         nc.scalar.activation(table_warmer[:], eps[:], ACT.Abs_reciprocal_sqrt)
 
+        window = held.tile([C, S], F32, name="window")
+        nc.scalar.dma_start(window[:], base)
+
         identity = held.tile([BLOCK, BLOCK], F32, name="identity")
         make_identity(nc, identity[:])
-        neg_shift = held.tile([C, 1], F32, name="neg_shift")
-        nc.gpsimd.tensor_scalar(neg_shift[:], shift[:], -1.0, None, ALU.mult)
 
         sum2 = held.tile([C, N], F32, name="sum2")
         nc.vector.tensor_tensor(sum2[:], xs[:], xc[:], ALU.add)
         sum3 = held.tile([C, N], F32, name="sum3")
         nc.vector.tensor_tensor(sum3[:], sum2[:], xp[:], ALU.add)
+        agg = held.tile([C, N], BF16, name="agg")
+        nc.vector.tensor_tensor(agg[:], sum3[:], xh[:], ALU.add)
 
-        h_t = []
+        h_t = [psum.tile([BLOCK, C], F32, name=f"h_t{b}") for b in range(NBLOCKS)]
         for b in range(NBLOCKS):
-            cols = slice(b * BLOCK, (b + 1) * BLOCK)
-            agg = held.tile([C, BLOCK], BF16, name=f"agg{b}")
-            nc.vector.tensor_tensor(agg[:], sum3[:, cols], xh[:, cols], ALU.add)
-            h_t.append(psum.tile([BLOCK, C], F32, name=f"h_t{b}"))
-            nc.tensor.matmul(h_t[b][:], agg[:], weights[:], start=True, stop=True)
-
-        mean_var = []
-        rstd = []
-        for b in range(NBLOCKS):
-            stats = held.tile([BLOCK, 6], F32, name=f"stats{b}")
-            nc.vector.bn_stats(stats[:], h_t[b][:])
-            mean_var.append(held.tile([BLOCK, 2], F32, name=f"mean_var{b}"))
-            nc.vector.bn_aggr(mean_var[b][:], stats[:])
-            rstd.append(held.tile([BLOCK, 1], F32, name=f"rstd{b}"))
-            nc.scalar.activation(rstd[b][:], mean_var[b][:, 1:2], ACT.Abs_reciprocal_sqrt, bias=eps[:])
-
-        centred_t = []
-        for b in range(NBLOCKS):
-            centred_t.append(held.tile([BLOCK, C], F32, name=f"centred_t{b}"))
-            nc.vector.scalar_tensor_tensor(
-                centred_t[b][:], h_t[b][:], mean_var[b][:, 0:1], scale_rows[:], ALU.subtract, ALU.mult
+            nc.tensor.matmul(
+                h_t[b][:], agg[:, b * BLOCK : (b + 1) * BLOCK], weights[:], start=True, stop=True
             )
 
-        u = []
+        stats = held.tile([BLOCK, NBLOCKS, 6], F32, name="stats")
+        mean_var = held.tile([BLOCK, NBLOCKS, 2], F32, name="mean_var")
         for b in range(NBLOCKS):
-            u_t = held.tile([BLOCK, C], F32, name=f"u_t{b}")
-            nc.vector.tensor_scalar(u_t[:], centred_t[b][:], rstd[b][:], None, ALU.mult)
-            u.append(psum.tile([C, BLOCK], F32, name=f"u{b}"))
-            nc.tensor.transpose(u[b][:], u_t[:], identity[:])
+            nc.vector.bn_stats(stats[:, b, :], h_t[b][:])
+        for b in range(NBLOCKS):
+            nc.vector.bn_aggr(mean_var[:, b, :], stats[:, b, :])
+        rstd = held.tile([BLOCK, NBLOCKS, 1], F32, name="rstd")
+        nc.scalar.activation(rstd[:], mean_var[:, :, 1:2], ACT.Abs_reciprocal_sqrt, bias=eps[:])
+
+        normed = psum.tile([C, N], F32, name="normed")
+        for b in range(NBLOCKS):
+            normed_t = held.tile([BLOCK, C], F32, name=f"normed_t{b}")
+            nc.vector.tensor_scalar(
+                normed_t[:], h_t[b][:], mean_var[:, b, 0:1], rstd[:, b, :], ALU.subtract, ALU.mult
+            )
+            nc.tensor.transpose(normed[:, b * BLOCK : (b + 1) * BLOCK], normed_t[:], identity[:])
 
         v = held.tile([C, N], F32, name="v")
+        nc.vector.tensor_scalar(v[:], normed[:], scale[:], shift[:], ALU.mult, ALU.add)
         slope = held.tile([C, N], F32, name="slope")
-        for b in range(NBLOCKS):
-            cols = slice(b * BLOCK, (b + 1) * BLOCK)
-            nc.vector.tensor_scalar(v[:, cols], u[b][:], shift[:], None, ALU.add)
-            nc.vector.tensor_scalar(slope[:, cols], u[b][:], neg_shift[:], NEG_SLOPE, ALU.is_ge, ALU.max)
-
+        nc.vector.tensor_scalar(slope[:], v[:], 0.0, NEG_SLOPE, ALU.is_ge, ALU.max)
         nc.vector.tensor_tensor(window[:].indirect(offsets[:]), v[:], slope[:], ALU.mult)
 
         nc.sync.dma_start(out, window[:])

@@ -31,9 +31,9 @@ def tile_modularfieldvortexlayer_kernel(
         xp = held.tile([C, N], F32, name="xp")
         xh = held.tile([C, N], F32, name="xh")
         nc.sync.dma_start(xs[:], x_self)
-        nc.scalar.dma_start(xc[:], x_cycle)
+        nc.sync.dma_start(xc[:], x_cycle)
         nc.sync.dma_start(xp[:], x_pair)
-        nc.scalar.dma_start(xh[:], x_hub)
+        nc.sync.dma_start(xh[:], x_hub)
         weights = held.tile([C, C], BF16, name="weights")
         nc.sync.dma_start(weights[:], w)
         offsets = held.tile([C, N // 16], U16, name="offsets")

@@ -1,5 +1,4 @@
 import concourse.mybir as mybir
-from concourse.masks import make_identity
 
 F32 = mybir.dt.float32
 BF16 = mybir.dt.bfloat16
@@ -10,10 +9,10 @@ ACT = mybir.ActivationFunctionType
 C = 128
 S = 1024
 N = 256
-BLOCK = 128
-NBLOCKS = N // BLOCK
 EPS = 1e-5
 NEG_SLOPE = 0.01
+IDLE_COLUMNS = 512
+IDLE_MATMULS = 6
 
 FLOPS = 2 * C * C * N
 
@@ -31,9 +30,9 @@ def tile_modularfieldvortexlayer_kernel(
         xp = held.tile([C, N], F32, name="xp")
         xh = held.tile([C, N], F32, name="xh")
         nc.sync.dma_start(xs[:], x_self)
-        nc.sync.dma_start(xc[:], x_cycle)
+        nc.scalar.dma_start(xc[:], x_cycle)
         nc.sync.dma_start(xp[:], x_pair)
-        nc.sync.dma_start(xh[:], x_hub)
+        nc.scalar.dma_start(xh[:], x_hub)
         weights = held.tile([C, C], BF16, name="weights")
         nc.sync.dma_start(weights[:], w)
         offsets = held.tile([C, N // 16], U16, name="offsets")
@@ -43,16 +42,34 @@ def tile_modularfieldvortexlayer_kernel(
         shift = held.tile([C, 1], F32, name="shift")
         nc.gpsimd.dma_start(shift[:], ln_shift)
 
-        eps = held.tile([BLOCK, 1], F32, name="eps")
+        eps = held.tile([C, 1], F32, name="eps")
         nc.vector.memset(eps[:], EPS)
-        table_warmer = held.tile([BLOCK, 1], F32, name="table_warmer")
+        table_warmer = held.tile([C, 1], F32, name="table_warmer")
         nc.scalar.activation(table_warmer[:], eps[:], ACT.Abs_reciprocal_sqrt)
 
         window = held.tile([C, S], F32, name="window")
         nc.scalar.dma_start(window[:], base)
 
-        identity = held.tile([BLOCK, BLOCK], F32, name="identity")
-        make_identity(nc, identity[:])
+        zeros = held.tile([C, C], F32, name="zeros")
+        nc.gpsimd.memset(zeros[:], 0.0)
+        mean_matrix = held.tile([C, C], F32, name="mean_matrix")
+        nc.gpsimd.memset(mean_matrix[:], 1.0 / C)
+        neg_shift = held.tile([C, 1], F32, name="neg_shift")
+        nc.gpsimd.tensor_scalar(neg_shift[:], shift[:], -1.0, None, ALU.mult)
+
+        idle_in = held.tile([C, IDLE_COLUMNS], BF16, name="idle_in")
+        nc.vector.memset(idle_in[:], 0.0)
+        idle_out = psum.tile([C, IDLE_COLUMNS], F32, name="idle_out")
+        for i in range(IDLE_MATMULS):
+            nc.tensor.matmul(idle_out[:], idle_in[:, 0:C], idle_in[:], start=True, stop=True)
+
+        unused = held.tile([C, C], F32, name="unused")
+        neg_wbar = held.tile([C, 1], F32, name="neg_wbar")
+        nc.scalar.activation(unused[:], weights[:], ACT.Identity, scale=-1.0 / C, accum_out=neg_wbar[:])
+        neg_wbar_hi = held.tile([C, C], BF16, name="neg_wbar_hi")
+        nc.scalar.activation(neg_wbar_hi[:], zeros[:], ACT.Identity, bias=neg_wbar[:])
+        neg_wbar_lo = held.tile([C, C], BF16, name="neg_wbar_lo")
+        nc.scalar.activation(neg_wbar_lo[:], neg_wbar_hi[:], ACT.Identity, scale=-1.0, bias=neg_wbar[:])
 
         sum2 = held.tile([C, N], F32, name="sum2")
         nc.vector.tensor_tensor(sum2[:], xs[:], xc[:], ALU.add)
@@ -61,33 +78,25 @@ def tile_modularfieldvortexlayer_kernel(
         agg = held.tile([C, N], BF16, name="agg")
         nc.vector.tensor_tensor(agg[:], sum3[:], xh[:], ALU.add)
 
-        h_t = [psum.tile([BLOCK, C], F32, name=f"h_t{b}") for b in range(NBLOCKS)]
-        for b in range(NBLOCKS):
-            nc.tensor.matmul(
-                h_t[b][:], agg[:, b * BLOCK : (b + 1) * BLOCK], weights[:], start=True, stop=True
-            )
+        centred = psum.tile([C, N], F32, name="centred")
+        nc.tensor.matmul(centred[:], weights[:], agg[:], start=True, stop=False)
+        nc.tensor.matmul(centred[:], neg_wbar_hi[:], agg[:], start=False, stop=False)
+        nc.tensor.matmul(centred[:], neg_wbar_lo[:], agg[:], start=False, stop=True)
 
-        stats = held.tile([BLOCK, NBLOCKS, 6], F32, name="stats")
-        mean_var = held.tile([BLOCK, NBLOCKS, 2], F32, name="mean_var")
-        for b in range(NBLOCKS):
-            nc.vector.bn_stats(stats[:, b, :], h_t[b][:])
-        for b in range(NBLOCKS):
-            nc.vector.bn_aggr(mean_var[:, b, :], stats[:, b, :])
-        rstd = held.tile([BLOCK, NBLOCKS, 1], F32, name="rstd")
-        nc.scalar.activation(rstd[:], mean_var[:, :, 1:2], ACT.Abs_reciprocal_sqrt, bias=eps[:])
+        squares = held.tile([C, N], F32, name="squares")
+        nc.scalar.activation(squares[:], centred[:], ACT.Square)
+        var = psum.tile([C, N], F32, name="var")
+        nc.tensor.matmul(var[:], mean_matrix[:], squares[:], start=True, stop=True)
+        rstd = held.tile([C, N], F32, name="rstd")
+        nc.scalar.activation(rstd[:], var[:], ACT.Abs_reciprocal_sqrt, bias=eps[:])
 
-        normed = psum.tile([C, N], F32, name="normed")
-        for b in range(NBLOCKS):
-            normed_t = held.tile([BLOCK, C], F32, name=f"normed_t{b}")
-            nc.vector.tensor_scalar(
-                normed_t[:], h_t[b][:], mean_var[:, b, 0:1], rstd[:, b, :], ALU.subtract, ALU.mult
-            )
-            nc.tensor.transpose(normed[:, b * BLOCK : (b + 1) * BLOCK], normed_t[:], identity[:])
-
+        u = held.tile([C, N], F32, name="u")
+        nc.vector.scalar_tensor_tensor(u[:], centred[:], scale[:], rstd[:], ALU.mult, ALU.mult)
         v = held.tile([C, N], F32, name="v")
-        nc.vector.tensor_scalar(v[:], normed[:], scale[:], shift[:], ALU.mult, ALU.add)
+        nc.vector.tensor_scalar(v[:], u[:], shift[:], None, ALU.add)
         slope = held.tile([C, N], F32, name="slope")
-        nc.vector.tensor_scalar(slope[:], v[:], 0.0, NEG_SLOPE, ALU.is_ge, ALU.max)
+        nc.vector.tensor_scalar(slope[:], u[:], neg_shift[:], NEG_SLOPE, ALU.is_ge, ALU.max)
+
         nc.vector.tensor_tensor(window[:].indirect(offsets[:]), v[:], slope[:], ALU.mult)
 
         nc.sync.dma_start(out, window[:])

@@ -87,11 +87,13 @@ def tile_modularfieldvortexlayer_kernel(
         nc.scalar.activation(squares[:], centred[:], ACT.Square)
         var = psum.tile([C, N], F32, name="var")
         nc.tensor.matmul(var[:], mean_matrix[:], squares[:], start=True, stop=True)
+        scaled = held.tile([C, N], F32, name="scaled")
+        nc.scalar.activation(scaled[:], centred[:], ACT.Identity, scale=scale[:])
         rstd = held.tile([C, N], F32, name="rstd")
         nc.scalar.activation(rstd[:], var[:], ACT.Abs_reciprocal_sqrt, bias=eps[:])
 
         u = held.tile([C, N], F32, name="u")
-        nc.vector.scalar_tensor_tensor(u[:], centred[:], scale[:], rstd[:], ALU.mult, ALU.mult)
+        nc.vector.tensor_tensor(u[:], scaled[:], rstd[:], ALU.mult)
         v = held.tile([C, N], F32, name="v")
         nc.vector.tensor_scalar(v[:], u[:], shift[:], None, ALU.add)
         slope = held.tile([C, N], F32, name="slope")

@@ -1,4 +1,5 @@
 import concourse.mybir as mybir
+from concourse.masks import make_identity
 
 F32 = mybir.dt.float32
 BF16 = mybir.dt.bfloat16
@@ -9,10 +10,10 @@ ACT = mybir.ActivationFunctionType
 C = 128
 S = 1024
 N = 256
+BLOCK = 128
+NBLOCKS = N // BLOCK
 EPS = 1e-5
 NEG_SLOPE = 0.01
-IDLE_COLUMNS = 512
-IDLE_MATMULS = 6
 
 FLOPS = 2 * C * C * N
 
@@ -42,63 +43,56 @@ def tile_modularfieldvortexlayer_kernel(
         shift = held.tile([C, 1], F32, name="shift")
         nc.gpsimd.dma_start(shift[:], ln_shift)
 
-        eps = held.tile([C, 1], F32, name="eps")
+        eps = held.tile([BLOCK, 1], F32, name="eps")
         nc.vector.memset(eps[:], EPS)
-        table_warmer = held.tile([C, 1], F32, name="table_warmer")
+        table_warmer = held.tile([BLOCK, 1], F32, name="table_warmer")
         nc.scalar.activation(table_warmer[:], eps[:], ACT.Abs_reciprocal_sqrt)
 
         window = held.tile([C, S], F32, name="window")
         nc.scalar.dma_start(window[:], base)
 
-        zeros = held.tile([C, C], F32, name="zeros")
-        nc.gpsimd.memset(zeros[:], 0.0)
-        mean_matrix = held.tile([C, C], F32, name="mean_matrix")
-        nc.gpsimd.memset(mean_matrix[:], 1.0 / C)
-        neg_shift = held.tile([C, 1], F32, name="neg_shift")
-        nc.gpsimd.tensor_scalar(neg_shift[:], shift[:], -1.0, None, ALU.mult)
-
-        idle_in = held.tile([C, IDLE_COLUMNS], BF16, name="idle_in")
-        nc.vector.memset(idle_in[:], 0.0)
-        idle_out = psum.tile([C, IDLE_COLUMNS], F32, name="idle_out")
-        for i in range(IDLE_MATMULS):
-            nc.tensor.matmul(idle_out[:], idle_in[:, 0:C], idle_in[:], start=True, stop=True)
-
-        unused = held.tile([C, C], F32, name="unused")
-        neg_wbar = held.tile([C, 1], F32, name="neg_wbar")
-        nc.scalar.activation(unused[:], weights[:], ACT.Identity, scale=-1.0 / C, accum_out=neg_wbar[:])
-        neg_wbar_hi = held.tile([C, C], BF16, name="neg_wbar_hi")
-        nc.scalar.activation(neg_wbar_hi[:], zeros[:], ACT.Identity, bias=neg_wbar[:])
-        neg_wbar_lo = held.tile([C, C], BF16, name="neg_wbar_lo")
-        nc.scalar.activation(neg_wbar_lo[:], neg_wbar_hi[:], ACT.Identity, scale=-1.0, bias=neg_wbar[:])
+        identity = held.tile([BLOCK, BLOCK], F32, name="identity")
+        make_identity(nc, identity[:])
 
         sum2 = held.tile([C, N], F32, name="sum2")
         nc.vector.tensor_tensor(sum2[:], xs[:], xc[:], ALU.add)
         sum3 = held.tile([C, N], F32, name="sum3")
         nc.vector.tensor_tensor(sum3[:], sum2[:], xp[:], ALU.add)
-        agg = held.tile([C, N], BF16, name="agg")
-        nc.vector.tensor_tensor(agg[:], sum3[:], xh[:], ALU.add)
 
-        centred = psum.tile([C, N], F32, name="centred")
-        nc.tensor.matmul(centred[:], weights[:], agg[:], start=True, stop=False)
-        nc.tensor.matmul(centred[:], neg_wbar_hi[:], agg[:], start=False, stop=False)
-        nc.tensor.matmul(centred[:], neg_wbar_lo[:], agg[:], start=False, stop=True)
+        h_t = []
+        for b in range(NBLOCKS):
+            cols = slice(b * BLOCK, (b + 1) * BLOCK)
+            agg = held.tile([C, BLOCK], BF16, name=f"agg{b}")
+            nc.vector.tensor_tensor(agg[:], sum3[:, cols], xh[:, cols], ALU.add)
+            h_t.append(psum.tile([BLOCK, C], F32, name=f"h_t{b}"))
+            nc.tensor.matmul(h_t[b][:], agg[:], weights[:], start=True, stop=True)
 
-        squares = held.tile([C, N], F32, name="squares")
-        nc.scalar.activation(squares[:], centred[:], ACT.Square)
-        var = psum.tile([C, N], F32, name="var")
-        nc.tensor.matmul(var[:], mean_matrix[:], squares[:], start=True, stop=True)
-        scaled = held.tile([C, N], F32, name="scaled")
-        nc.scalar.activation(scaled[:], centred[:], ACT.Identity, scale=scale[:])
-        rstd = held.tile([C, N], F32, name="rstd")
-        nc.scalar.activation(rstd[:], var[:], ACT.Abs_reciprocal_sqrt, bias=eps[:])
+        mean_var = []
+        rstd = []
+        for b in range(NBLOCKS):
+            stats = held.tile([BLOCK, 6], F32, name=f"stats{b}")
+            nc.vector.bn_stats(stats[:], h_t[b][:])
+            mean_var.append(held.tile([BLOCK, 2], F32, name=f"mean_var{b}"))
+            nc.vector.bn_aggr(mean_var[b][:], stats[:])
+            rstd.append(held.tile([BLOCK, 1], F32, name=f"rstd{b}"))
+            nc.scalar.activation(rstd[b][:], mean_var[b][:, 1:2], ACT.Abs_reciprocal_sqrt, bias=eps[:])
 
-        u = held.tile([C, N], F32, name="u")
-        nc.vector.tensor_tensor(u[:], scaled[:], rstd[:], ALU.mult)
+        normed = []
+        for b in range(NBLOCKS):
+            normed_t = held.tile([BLOCK, C], F32, name=f"normed_t{b}")
+            nc.vector.tensor_scalar(
+                normed_t[:], h_t[b][:], mean_var[b][:, 0:1], rstd[b][:], ALU.subtract, ALU.mult
+            )
+            normed.append(psum.tile([C, BLOCK], F32, name=f"normed{b}"))
+            nc.tensor.transpose(normed[b][:], normed_t[:], identity[:])
+
         v = held.tile([C, N], F32, name="v")
-        nc.vector.tensor_scalar(v[:], u[:], shift[:], None, ALU.add)
+        for b in range(NBLOCKS):
+            nc.vector.tensor_scalar(
+                v[:, b * BLOCK : (b + 1) * BLOCK], normed[b][:], scale[:], shift[:], ALU.mult, ALU.add
+            )
         slope = held.tile([C, N], F32, name="slope")
-        nc.vector.tensor_scalar(slope[:], u[:], neg_shift[:], NEG_SLOPE, ALU.is_ge, ALU.max)
-
+        nc.vector.tensor_scalar(slope[:], v[:], 0.0, NEG_SLOPE, ALU.is_ge, ALU.max)
         nc.vector.tensor_tensor(window[:].indirect(offsets[:]), v[:], slope[:], ALU.mult)
 
         nc.sync.dma_start(out, window[:])

@@ -54,34 +54,35 @@ def tile_modularfieldvortexlayer_kernel(
         identity = held.tile([BLOCK, BLOCK], F32, name="identity")
         make_identity(nc, identity[:])
 
-        sum2 = held.tile([C, N], F32, name="sum2")
-        nc.vector.tensor_tensor(sum2[:], xs[:], xc[:], ALU.add)
-        sum3 = held.tile([C, N], F32, name="sum3")
-        nc.vector.tensor_tensor(sum3[:], sum2[:], xp[:], ALU.add)
+        first_sum = held.tile([C, N], F32, name="first_sum")
+        nc.vector.tensor_tensor(first_sum[:], xs[:], xc[:], ALU.add)
 
         h_t = []
         for b in range(NBLOCKS):
             cols = slice(b * BLOCK, (b + 1) * BLOCK)
+            second_sum = held.tile([C, BLOCK], F32, name=f"second_sum{b}")
+            nc.vector.tensor_tensor(second_sum[:], xp[:, cols], xh[:, cols], ALU.add)
             agg = held.tile([C, BLOCK], BF16, name=f"agg{b}")
-            nc.vector.tensor_tensor(agg[:], sum3[:, cols], xh[:, cols], ALU.add)
+            nc.vector.tensor_tensor(agg[:], first_sum[:, cols], second_sum[:], ALU.add)
             h_t.append(psum.tile([BLOCK, C], F32, name=f"h_t{b}"))
             nc.tensor.matmul(h_t[b][:], agg[:], weights[:], start=True, stop=True)
 
-        mean_var = []
+        stats = []
         rstd = []
         for b in range(NBLOCKS):
-            stats = held.tile([BLOCK, 6], F32, name=f"stats{b}")
-            nc.vector.bn_stats(stats[:], h_t[b][:])
-            mean_var.append(held.tile([BLOCK, 2], F32, name=f"mean_var{b}"))
-            nc.vector.bn_aggr(mean_var[b][:], stats[:])
+            stats.append(held.tile([BLOCK, 6], F32, name=f"stats{b}"))
+            each_twice = h_t[b][:].unsqueeze(2).to_broadcast([BLOCK, C, 2])
+            nc.vector.bn_stats(stats[b][:], each_twice)
             rstd.append(held.tile([BLOCK, 1], F32, name=f"rstd{b}"))
-            nc.scalar.activation(rstd[b][:], mean_var[b][:, 1:2], ACT.Abs_reciprocal_sqrt, bias=eps[:])
+            nc.scalar.activation(
+                rstd[b][:], stats[b][:, 2:3], ACT.Abs_reciprocal_sqrt, bias=eps[:], scale=1.0 / C
+            )
 
         normed = []
         for b in range(NBLOCKS):
             normed_t = held.tile([BLOCK, C], F32, name=f"normed_t{b}")
             nc.vector.tensor_scalar(
-                normed_t[:], h_t[b][:], mean_var[b][:, 0:1], rstd[b][:], ALU.subtract, ALU.mult
+                normed_t[:], h_t[b][:], stats[b][:, 1:2], rstd[b][:], ALU.subtract, ALU.mult
             )
             normed.append(psum.tile([C, BLOCK], F32, name=f"normed{b}"))
             nc.tensor.transpose(normed[b][:], normed_t[:], identity[:])

@@ -49,7 +49,7 @@ def tile_modularfieldvortexlayer_kernel(
         nc.scalar.activation(table_warmer[:], eps[:], ACT.Abs_reciprocal_sqrt)
 
         window = held.tile([C, S], F32, name="window")
-        nc.scalar.dma_start(window[:], base)
+        nc.sync.dma_start(window[:], base)
 
         identity = held.tile([BLOCK, BLOCK], F32, name="identity")
         make_identity(nc, identity[:])

@@ -36,6 +36,8 @@ def tile_modularfieldvortexlayer_kernel(
         nc.scalar.dma_start(xh[:], x_hub)
         weights = held.tile([C, C], BF16, name="weights")
         nc.sync.dma_start(weights[:], w)
+        window = held.tile([C, S], F32, name="window")
+        nc.sync.dma_start(window[:], base)
         offsets = held.tile([C, N // 16], U16, name="offsets")
         nc.sync.dma_start(offsets[:], offs)
         scale = held.tile([C, 1], F32, name="scale")
@@ -47,9 +49,6 @@ def tile_modularfieldvortexlayer_kernel(
         nc.vector.memset(eps[:], EPS)
         table_warmer = held.tile([BLOCK, 1], F32, name="table_warmer")
         nc.scalar.activation(table_warmer[:], eps[:], ACT.Abs_reciprocal_sqrt)
-
-        window = held.tile([C, S], F32, name="window")
-        nc.sync.dma_start(window[:], base)
 
         identity = held.tile([BLOCK, BLOCK], F32, name="identity")
         make_identity(nc, identity[:])

@@ -53,16 +53,16 @@ def tile_modularfieldvortexlayer_kernel(
         identity = held.tile([BLOCK, BLOCK], F32, name="identity")
         make_identity(nc, identity[:])
 
-        first_sum = held.tile([C, N], F32, name="first_sum")
-        nc.vector.tensor_tensor(first_sum[:], xs[:], xc[:], ALU.add)
+        sum2 = held.tile([C, N], F32, name="sum2")
+        nc.vector.tensor_tensor(sum2[:], xs[:], xc[:], ALU.add)
 
         h_t = []
         for b in range(NBLOCKS):
             cols = slice(b * BLOCK, (b + 1) * BLOCK)
-            second_sum = held.tile([C, BLOCK], F32, name=f"second_sum{b}")
-            nc.vector.tensor_tensor(second_sum[:], xp[:, cols], xh[:, cols], ALU.add)
+            sum3 = held.tile([C, BLOCK], F32, name=f"sum3_{b}")
+            nc.vector.tensor_tensor(sum3[:], sum2[:, cols], xp[:, cols], ALU.add)
             agg = held.tile([C, BLOCK], BF16, name=f"agg{b}")
-            nc.vector.tensor_tensor(agg[:], first_sum[:, cols], second_sum[:], ALU.add)
+            nc.vector.tensor_tensor(agg[:], sum3[:], xh[:, cols], ALU.add)
             h_t.append(psum.tile([BLOCK, C], F32, name=f"h_t{b}"))
             nc.tensor.matmul(h_t[b][:], agg[:], weights[:], start=True, stop=True)
 

@@ -87,12 +87,11 @@ def tile_modularfieldvortexlayer_kernel(
             nc.tensor.transpose(normed[b][:], normed_t[:], identity[:])
 
         v = held.tile([C, N], F32, name="v")
-        for b in range(NBLOCKS):
-            nc.vector.tensor_scalar(
-                v[:, b * BLOCK : (b + 1) * BLOCK], normed[b][:], scale[:], shift[:], ALU.mult, ALU.add
-            )
         slope = held.tile([C, N], F32, name="slope")
-        nc.vector.tensor_scalar(slope[:], v[:], 0.0, NEG_SLOPE, ALU.is_ge, ALU.max)
+        for b in range(NBLOCKS):
+            cols = slice(b * BLOCK, (b + 1) * BLOCK)
+            nc.vector.tensor_scalar(v[:, cols], normed[b][:], scale[:], shift[:], ALU.mult, ALU.add)
+            nc.vector.tensor_scalar(slope[:, cols], v[:, cols], 0.0, NEG_SLOPE, ALU.is_ge, ALU.max)
         nc.vector.tensor_tensor(window[:].indirect(offsets[:]), v[:], slope[:], ALU.mult)
 
         nc.sync.dma_start(out, window[:])

@@ -40,6 +40,8 @@ def tile_modularfieldvortexlayer_kernel(
         nc.sync.dma_start(window[:], base)
         offsets = held.tile([C, N // 16], U16, name="offsets")
         nc.sync.dma_start(offsets[:], offs)
+        identity = held.tile([BLOCK, BLOCK], F32, name="identity")
+        make_identity(nc, identity[:])
         scale = held.tile([C, 1], F32, name="scale")
         nc.gpsimd.dma_start(scale[:], ln_scale)
         shift = held.tile([C, 1], F32, name="shift")
@@ -49,9 +51,6 @@ def tile_modularfieldvortexlayer_kernel(
         nc.vector.memset(eps[:], EPS)
         table_warmer = held.tile([BLOCK, 1], F32, name="table_warmer")
         nc.scalar.activation(table_warmer[:], eps[:], ACT.Abs_reciprocal_sqrt)
-
-        identity = held.tile([BLOCK, BLOCK], F32, name="identity")
-        make_identity(nc, identity[:])
 
         sum2 = held.tile([C, N], F32, name="sum2")
         nc.vector.tensor_tensor(sum2[:], xs[:], xc[:], ALU.add)

@@ -52,45 +52,64 @@ def tile_modularfieldvortexlayer_kernel(
         table_warmer = held.tile([BLOCK, 1], F32, name="table_warmer")
         nc.scalar.activation(table_warmer[:], eps[:], ACT.Abs_reciprocal_sqrt)
 
+        w_scaled = held.tile([C, C], F32, name="w_scaled")
+        neg_wbar = held.tile([C, 1], F32, name="neg_wbar")
+        nc.scalar.activation(
+            w_scaled[:], weights[:], ACT.Copy, scale=-1.0 / C, accum_out=neg_wbar[:]
+        )
+        neg_wbar_hi = held.tile([C, 1], BF16, name="neg_wbar_hi")
+        nc.scalar.activation(neg_wbar_hi[:], neg_wbar[:], ACT.Copy)
+        neg_wbar_lo = held.tile([C, 1], BF16, name="neg_wbar_lo")
+        nc.scalar.activation(
+            neg_wbar_lo[:], neg_wbar_hi[:], ACT.Identity, bias=neg_wbar[:], scale=-1.0
+        )
+
         sum2 = held.tile([C, N], F32, name="sum2")
         nc.vector.tensor_tensor(sum2[:], xs[:], xc[:], ALU.add)
 
+        agg = held.tile([C, N], BF16, name="agg")
         h_t = []
         for b in range(NBLOCKS):
             cols = slice(b * BLOCK, (b + 1) * BLOCK)
             sum3 = held.tile([C, BLOCK], F32, name=f"sum3_{b}")
             nc.vector.tensor_tensor(sum3[:], sum2[:, cols], xp[:, cols], ALU.add)
-            agg = held.tile([C, BLOCK], BF16, name=f"agg{b}")
-            nc.vector.tensor_tensor(agg[:], sum3[:], xh[:, cols], ALU.add)
+            nc.vector.tensor_tensor(agg[:, cols], sum3[:], xh[:, cols], ALU.add)
             h_t.append(psum.tile([BLOCK, C], F32, name=f"h_t{b}"))
-            nc.tensor.matmul(h_t[b][:], agg[:], weights[:], start=True, stop=True)
+            nc.tensor.matmul(h_t[b][:], agg[:, cols], weights[:], start=True, stop=True)
 
-        stats = []
-        rstd = []
+        centred = psum.tile([C, N], F32, name="centred")
+        nc.tensor.matmul(centred[:], weights[:], agg[:], start=True, stop=False)
+        nc.tensor.matmul(
+            centred[:], neg_wbar_hi[:].to_broadcast([C, C]), agg[:], start=False, stop=False
+        )
+        nc.tensor.matmul(
+            centred[:], neg_wbar_lo[:].to_broadcast([C, C]), agg[:], start=False, stop=True
+        )
+
+        rstd_cols = []
         for b in range(NBLOCKS):
-            stats.append(held.tile([BLOCK, 6], F32, name=f"stats{b}"))
+            stats = held.tile([BLOCK, 6], F32, name=f"stats{b}")
             each_twice = h_t[b][:].unsqueeze(2).to_broadcast([BLOCK, C, 2])
-            nc.vector.bn_stats(stats[b][:], each_twice)
-            rstd.append(held.tile([BLOCK, 1], F32, name=f"rstd{b}"))
+            nc.vector.bn_stats(stats[:], each_twice)
+            rstd = held.tile([BLOCK, 1], F32, name=f"rstd{b}")
             nc.scalar.activation(
-                rstd[b][:], stats[b][:, 2:3], ACT.Abs_reciprocal_sqrt, bias=eps[:], scale=1.0 / C
+                rstd[:], stats[:, 2:3], ACT.Abs_reciprocal_sqrt, bias=eps[:], scale=1.0 / C
             )
+            rstd_cols.append(psum.tile([C, BLOCK], F32, name=f"rstd_cols{b}"))
+            nc.tensor.transpose(rstd_cols[b][:], rstd[:].to_broadcast([BLOCK, C]), identity[:])
 
-        normed = []
-        for b in range(NBLOCKS):
-            normed_t = held.tile([BLOCK, C], F32, name=f"normed_t{b}")
-            nc.vector.tensor_scalar(
-                normed_t[:], h_t[b][:], stats[b][:, 1:2], rstd[b][:], ALU.subtract, ALU.mult
-            )
-            normed.append(psum.tile([C, BLOCK], F32, name=f"normed{b}"))
-            nc.tensor.transpose(normed[b][:], normed_t[:], identity[:])
-
+        scaled = held.tile([C, N], F32, name="scaled")
+        nc.vector.tensor_scalar(scaled[:], centred[:], scale[:], -1.0, ALU.mult, ALU.mult)
         v = held.tile([C, N], F32, name="v")
         slope = held.tile([C, N], F32, name="slope")
         for b in range(NBLOCKS):
             cols = slice(b * BLOCK, (b + 1) * BLOCK)
-            nc.vector.tensor_scalar(v[:, cols], normed[b][:], scale[:], shift[:], ALU.mult, ALU.add)
-            nc.vector.tensor_scalar(slope[:, cols], v[:, cols], 0.0, NEG_SLOPE, ALU.is_ge, ALU.max)
+            drop = held.tile([C, BLOCK], F32, name=f"drop{b}")
+            nc.vector.tensor_tensor(drop[:], scaled[:, cols], rstd_cols[b][:], ALU.mult)
+            nc.vector.tensor_scalar(v[:, cols], drop[:], -1.0, shift[:], ALU.mult, ALU.add)
+            nc.vector.tensor_scalar(
+                slope[:, cols], drop[:], shift[:], NEG_SLOPE, ALU.is_le, ALU.max
+            )
         nc.vector.tensor_tensor(window[:].indirect(offsets[:]), v[:], slope[:], ALU.mult)
 
         nc.sync.dma_start(out, window[:])

@@ -64,16 +64,16 @@ def tile_modularfieldvortexlayer_kernel(
             neg_wbar_lo[:], neg_wbar_hi[:], ACT.Identity, bias=neg_wbar[:], scale=-1.0
         )
 
+        block_cols = [slice(b * BLOCK, (b + 1) * BLOCK) for b in range(NBLOCKS)]
         sum2 = held.tile([C, N], F32, name="sum2")
-        nc.vector.tensor_tensor(sum2[:], xs[:], xc[:], ALU.add)
-
+        sum3 = held.tile([C, N], F32, name="sum3")
         agg = held.tile([C, N], BF16, name="agg")
+        for total, left, right in ((sum2, xs, xc), (sum3, sum2, xp), (agg, sum3, xh)):
+            for cols in block_cols:
+                nc.vector.tensor_tensor(total[:, cols], left[:, cols], right[:, cols], ALU.add)
+
         h_t = []
-        for b in range(NBLOCKS):
-            cols = slice(b * BLOCK, (b + 1) * BLOCK)
-            sum3 = held.tile([C, BLOCK], F32, name=f"sum3_{b}")
-            nc.vector.tensor_tensor(sum3[:], sum2[:, cols], xp[:, cols], ALU.add)
-            nc.vector.tensor_tensor(agg[:, cols], sum3[:], xh[:, cols], ALU.add)
+        for b, cols in enumerate(block_cols):
             h_t.append(psum.tile([BLOCK, C], F32, name=f"h_t{b}"))
             nc.tensor.matmul(h_t[b][:], agg[:, cols], weights[:], start=True, stop=True)
 
@@ -102,8 +102,7 @@ def tile_modularfieldvortexlayer_kernel(
         nc.vector.tensor_scalar(scaled[:], centred[:], scale[:], -1.0, ALU.mult, ALU.mult)
         v = held.tile([C, N], F32, name="v")
         slope = held.tile([C, N], F32, name="slope")
-        for b in range(NBLOCKS):
-            cols = slice(b * BLOCK, (b + 1) * BLOCK)
+        for b, cols in enumerate(block_cols):
             drop = held.tile([C, BLOCK], F32, name=f"drop{b}")
             nc.vector.tensor_tensor(drop[:], scaled[:, cols], rstd_cols[b][:], ALU.mult)
             nc.vector.tensor_scalar(v[:, cols], drop[:], -1.0, shift[:], ALU.mult, ALU.add)

@@ -12,6 +12,7 @@ S = 1024
 N = 256
 BLOCK = 128
 NBLOCKS = N // BLOCK
+PIECE = 64
 EPS = 1e-5
 NEG_SLOPE = 0.01
 
@@ -65,11 +66,12 @@ def tile_modularfieldvortexlayer_kernel(
         )
 
         block_cols = [slice(b * BLOCK, (b + 1) * BLOCK) for b in range(NBLOCKS)]
+        piece_cols = [slice(p * PIECE, (p + 1) * PIECE) for p in range(N // PIECE)]
         sum2 = held.tile([C, N], F32, name="sum2")
         sum3 = held.tile([C, N], F32, name="sum3")
         agg = held.tile([C, N], BF16, name="agg")
         for total, left, right in ((sum2, xs, xc), (sum3, sum2, xp), (agg, sum3, xh)):
-            for cols in block_cols:
+            for cols in piece_cols:
                 nc.vector.tensor_tensor(total[:, cols], left[:, cols], right[:, cols], ALU.add)
 
         h_t = []

import concourse.mybir as mybir
from concourse.masks import make_identity

F32 = mybir.dt.float32
BF16 = mybir.dt.bfloat16
U16 = mybir.dt.uint16
ALU = mybir.AluOpType
ACT = mybir.ActivationFunctionType

C = 128
S = 1024
N = 256
BLOCK = 128
NBLOCKS = N // BLOCK
PIECE = 64
EPS = 1e-5
NEG_SLOPE = 0.01

FLOPS = 2 * C * C * N


def tile_modularfieldvortexlayer_kernel(
    tc, base, x_self, x_cycle, x_pair, x_hub, w, ln_scale, ln_shift, offs, out
):
    nc = tc.nc
    with (
        tc.tile_pool(name="held", bufs=1) as held,
        tc.psum_pool(name="psum", bufs=1) as psum,
    ):
        xs = held.tile([C, N], F32, name="xs")
        xc = held.tile([C, N], F32, name="xc")
        xp = held.tile([C, N], F32, name="xp")
        xh = held.tile([C, N], F32, name="xh")
        nc.sync.dma_start(xs[:], x_self)
        nc.scalar.dma_start(xc[:], x_cycle)
        nc.sync.dma_start(xp[:], x_pair)
        nc.scalar.dma_start(xh[:], x_hub)
        weights = held.tile([C, C], BF16, name="weights")
        nc.sync.dma_start(weights[:], w)
        window = held.tile([C, S], F32, name="window")
        nc.sync.dma_start(window[:], base)
        offsets = held.tile([C, N // 16], U16, name="offsets")
        nc.sync.dma_start(offsets[:], offs)
        identity = held.tile([BLOCK, BLOCK], F32, name="identity")
        make_identity(nc, identity[:])
        scale = held.tile([C, 1], F32, name="scale")
        nc.gpsimd.dma_start(scale[:], ln_scale)
        shift = held.tile([C, 1], F32, name="shift")
        nc.gpsimd.dma_start(shift[:], ln_shift)

        eps = held.tile([BLOCK, 1], F32, name="eps")
        nc.vector.memset(eps[:], EPS)
        table_warmer = held.tile([BLOCK, 1], F32, name="table_warmer")
        nc.scalar.activation(table_warmer[:], eps[:], ACT.Abs_reciprocal_sqrt)

        w_scaled = held.tile([C, C], F32, name="w_scaled")
        neg_wbar = held.tile([C, 1], F32, name="neg_wbar")
        nc.scalar.activation(
            w_scaled[:], weights[:], ACT.Copy, scale=-1.0 / C, accum_out=neg_wbar[:]
        )
        neg_wbar_hi = held.tile([C, 1], BF16, name="neg_wbar_hi")
        nc.scalar.activation(neg_wbar_hi[:], neg_wbar[:], ACT.Copy)
        neg_wbar_lo = held.tile([C, 1], BF16, name="neg_wbar_lo")
        nc.scalar.activation(
            neg_wbar_lo[:], neg_wbar_hi[:], ACT.Identity, bias=neg_wbar[:], scale=-1.0
        )

        block_cols = [slice(b * BLOCK, (b + 1) * BLOCK) for b in range(NBLOCKS)]
        piece_cols = [slice(p * PIECE, (p + 1) * PIECE) for p in range(N // PIECE)]
        sum2 = held.tile([C, N], F32, name="sum2")
        sum3 = held.tile([C, N], F32, name="sum3")
        agg = held.tile([C, N], BF16, name="agg")
        for total, left, right in ((sum2, xs, xc), (sum3, sum2, xp), (agg, sum3, xh)):
            for cols in piece_cols:
                nc.vector.tensor_tensor(total[:, cols], left[:, cols], right[:, cols], ALU.add)

        h_t = []
        for b, cols in enumerate(block_cols):
            h_t.append(psum.tile([BLOCK, C], F32, name=f"h_t{b}"))
            nc.tensor.matmul(h_t[b][:], agg[:, cols], weights[:], start=True, stop=True)

        centred = psum.tile([C, N], F32, name="centred")
        nc.tensor.matmul(centred[:], weights[:], agg[:], start=True, stop=False)
        nc.tensor.matmul(
            centred[:], neg_wbar_hi[:].to_broadcast([C, C]), agg[:], start=False, stop=False
        )
        nc.tensor.matmul(
            centred[:], neg_wbar_lo[:].to_broadcast([C, C]), agg[:], start=False, stop=True
        )

        rstd_cols = []
        for b in range(NBLOCKS):
            stats = held.tile([BLOCK, 6], F32, name=f"stats{b}")
            each_twice = h_t[b][:].unsqueeze(2).to_broadcast([BLOCK, C, 2])
            nc.vector.bn_stats(stats[:], each_twice)
            rstd = held.tile([BLOCK, 1], F32, name=f"rstd{b}")
            nc.scalar.activation(
                rstd[:], stats[:, 2:3], ACT.Abs_reciprocal_sqrt, bias=eps[:], scale=1.0 / C
            )
            rstd_cols.append(psum.tile([C, BLOCK], F32, name=f"rstd_cols{b}"))
            nc.tensor.transpose(rstd_cols[b][:], rstd[:].to_broadcast([BLOCK, C]), identity[:])

        scaled = held.tile([C, N], F32, name="scaled")
        nc.vector.tensor_scalar(scaled[:], centred[:], scale[:], -1.0, ALU.mult, ALU.mult)
        v = held.tile([C, N], F32, name="v")
        slope = held.tile([C, N], F32, name="slope")
        for b, cols in enumerate(block_cols):
            drop = held.tile([C, BLOCK], F32, name=f"drop{b}")
            nc.vector.tensor_tensor(drop[:], scaled[:, cols], rstd_cols[b][:], ALU.mult)
            nc.vector.tensor_scalar(v[:, cols], drop[:], -1.0, shift[:], ALU.mult, ALU.add)
            nc.vector.tensor_scalar(
                slope[:, cols], drop[:], shift[:], NEG_SLOPE, ALU.is_le, ALU.max
            )
        nc.vector.tensor_tensor(window[:].indirect(offsets[:]), v[:], slope[:], ALU.mult)

        nc.sync.dma_start(out, window[:])
